import numpy as np
import ml_dtypes


def mxq(x, axis, fmt="e4m3"):
    dtype, down = {"e4m3": (ml_dtypes.float8_e4m3fn, 7), "e5m2": (ml_dtypes.float8_e5m2, 14)}[fmt]
    v = np.moveaxis(np.asarray(x, np.float32).astype(ml_dtypes.bfloat16).astype(np.float64), axis, -1)
    blocks = v.reshape(v.shape[:-1] + (-1, 32))
    amax = np.abs(blocks).max(-1, keepdims=True)
    byte = np.maximum(np.where(amax > 0, np.frexp(amax)[1] - 1 + 127, 0) - down, 1)
    scale = np.exp2(byte - 127.0)
    codes = (blocks / scale).astype(np.float32).astype(dtype).astype(np.float64)
    return np.moveaxis((codes * scale).reshape(v.shape), -1, axis)


WIDE = False


def mx_kscale(k):
    if not WIDE:
        return np.ones(k)
    levels = np.array([10, -10, 5, -5, 0])
    if k % 512:
        return np.exp2(np.random.permutation(np.resize(levels, k // 32))).repeat(32)
    a = np.empty((k // 512, 16))
    for p in range(k // 512):
        a[p, :8] = np.random.permutation(np.resize(levels, 8))
        for g in range(8):
            far = levels[np.abs(levels - a[p, g]) >= 10]
            a[p, g + 8] = far[np.random.randint(len(far))]
    return np.exp2(a.ravel()).repeat(32)


BF16 = ml_dtypes.bfloat16


def bf(x):
    return np.asarray(x, np.float32).astype(BF16)


def f64(x):
    return np.asarray(x).astype(np.float64)


B, N, NIN, CTX, H, NOUT = 2, 512, 512, 3, 1024, 2
F = NIN * CTX


def shift_down(y, d):
    return np.pad(y[:, :-d, :], ((0, 0), (d, 0), (0, 0)))


def shift_up(y, d):
    return np.pad(y[:, d:, :], ((0, 0), (0, d), (0, 0)))


def context_linear(xq, w, shifts):
    y = f64(bf(xq @ mxq(w[:, :NIN].T, 0, "e4m3")))
    c = 1
    for d in range(1, CTX // 2 + 1):
        for shift in shifts:
            y = y + shift(f64(bf(xq @ mxq(w[:, c * NIN:(c + 1) * NIN].T, 0, "e4m3"))), d)
            c += 1
    return y


def setup_inputs():
    s, u = mx_kscale(NIN), mx_kscale(H)
    return {"t_bil": bf(np.random.standard_normal((B, N, NOUT, H)) * 0.15 / u),
            "x_r": bf(np.random.standard_normal((B, N, NIN)) * s),
            "W_r": bf(np.random.standard_normal((H, F)) / np.sqrt(F) / np.tile(s, CTX) * u[:, None]),
            "b_r": bf(np.random.standard_normal(H) * 0.3 * u),
            "b_bil": bf(np.random.standard_normal(NOUT))}


def reference(t_bil, x_r, W_r, b_r, b_bil):
    xq = mxq(f64(x_r), 2, "e4m3")
    hr = np.maximum(context_linear(xq, f64(W_r), (shift_up, shift_down)) + f64(b_r), 0.0)
    tq = mxq(f64(t_bil).reshape(B, N * NOUT, H), 2, "e4m3")
    sc = tq @ mxq(hr.transpose(0, 2, 1), 1, "e4m3")
    return sc.reshape(B, N, NOUT, N).transpose(0, 1, 3, 2) + f64(b_bil)

@@ -1,0 +1,219 @@
+from contextlib import ExitStack
+
+import concourse.mybir as mybir
+from concourse.masks import make_identity
+
+F32 = mybir.dt.float32
+BF16 = mybir.dt.bfloat16
+U32 = mybir.dt.uint32
+U8 = mybir.dt.uint8
+FP8X4 = mybir.dt.float8_e4m3fn_x4
+ADD = mybir.AluOpType.add
+RELU = mybir.ActivationFunctionType.Relu
+IDENTITY = mybir.ActivationFunctionType.Identity
+
+P = 128
+FLOPS = 3 * 2 * 1024 * 1024 * 512 + 2 * 2 * 1024 * 512 * 1024
+MAX_RUN = 16
+SPLIT = 256
+
+BANK_DT = BF16
+
+
+def tile_bilinearpairedlayer_pb_kernel(tc, t_bil, x_r, W_r, b_r, b_bil, out):
+    nc = tc.nc
+    with ExitStack() as ctx:
+        keep = ctx.enter_context(tc.tile_pool(name="keep", bufs=1))
+        work = ctx.enter_context(tc.tile_pool(name="work", bufs=2))
+        psum = ctx.enter_context(tc.psum_pool(name="psum", bufs=8))
+        ctx.enter_context(tc.manual_schedule())
+
+        x_sb = [keep.tile([P, 4, 512], BF16, name="x_sb%d" % b) for b in range(2)]
+        w_sb = [keep.tile([P, 2, 1536], BF16, name="w_sb%d" % u) for u in range(4)]
+        t_sb = [[keep.tile([P, 2, 1024], BF16, name="t_sb%d%d" % (b, it)) for it in range(4)] for b in range(2)]
+        w_view = W_r.rearrange("(G m h t) c -> G h m t c", G=2, m=P, h=2, t=2)
+
+        def load_x(b):
+            x_view = x_r[b].rearrange("(r p) f -> p r f", p=P)
+            for h in range(2):
+                nc.sync.dma_start(out=x_sb[b][:, 2 * h : 2 * h + 2, :], in_=x_view[:, 2 * h : 2 * h + 2, :])
+
+        def load_w(u, pieces):
+            for cs in pieces:
+                nc.sync.dma_start(out=w_sb[u][:, :, cs], in_=w_view[u // 2, u % 2][:, :, cs])
+
+        def load_t(b, it):
+            nc.sync.dma_start(out=t_sb[b][it][:], in_=t_bil[b, it * P : (it + 1) * P])
+
+        load_x(0)
+        load_w(0, [slice(512 * c, 512 * (c + 1)) for c in (1, 0, 2)])
+        for u in (1, 2, 3):
+            load_w(u, [slice(0, 1536)])
+        load_x(1)
+        for b in range(2):
+            for it in range(4):
+                load_t(b, it)
+
+        br = keep.tile([P, 2, 4], BF16, name="br")
+        bb = keep.tile([P, 2], BF16, name="bb")
+        with nc.allow_non_contiguous_dma(reason="two small bias vectors"):
+            nc.scalar.dma_start(out=br[:], in_=b_r.rearrange("(G p t) -> p G t", G=2, t=4))
+            nc.scalar.dma_start(out=bb[:], in_=b_bil.partition_broadcast(P))
+
+        warm = keep.tile([P, 2], F32, name="warm")
+        nc.vector.memset(warm[:], 0.0)
+        nc.scalar.activation(out=warm[:, 1:2], in_=warm[:, 0:1], func=RELU)
+
+        ident = keep.tile([P, P], F32, name="ident")
+        make_identity(nc, ident[:])
+
+        zero = keep.tile([P, 256], F32, name="zero")
+        nc.gpsimd.memset(zero[:], 0.0)
+        bias2 = keep.tile([P, 256, 2], F32, name="bias2")
+        for k in range(2):
+            nc.gpsimd.tensor_scalar(out=bias2[:, :, k], in0=zero[:], scalar1=bb[:, k : k + 1], scalar2=None, op0=ADD)
+
+        y1_sb = [keep.tile([P, 520], BANK_DT, name="y1_sb%d" % n) for n in range(4)]
+        for n in range(4):
+            nc.vector.memset(y1_sb[n][:, 512:520], 0.0)
+
+        xq = keep.tile([P, 1024], U32, name="xq", align_bytes=64)
+        xs = keep.tile([P, 1024], U8, name="xs", align_bytes=64)
+        wq = keep.tile([P, 3, 1024], U32, name="wq", align_bytes=64)
+        ws = keep.tile([P, 3, 1024], U8, name="ws", align_bytes=64)
+        tq = [keep.tile([P, 2048], U32, name="tq%d" % b, align_bytes=64) for b in range(2)]
+        ts = [keep.tile([P, 2048], U8, name="ts%d" % b, align_bytes=64) for b in range(2)]
+        hq = [keep.tile([P, 2, 512], U32, name="hq%d" % b, align_bytes=64) for b in range(2)]
+        hs = [keep.tile([P, 2, 512], U8, name="hs%d" % b, align_bytes=64) for b in range(2)]
+
+        def turn(blocks, grouped):
+            bank = psum.tile([P, 2, 2, P], F32, name="turned", tag="bank")
+            for i in range(2):
+                words = blocks[i].bitcast(F32)
+                for u in range(2):
+                    nc.tensor.transpose(bank[:, i, u, :], words[:, u:256:2], ident[:])
+            dst = grouped.rearrange("p c j -> p (c j)").bitcast(F32).rearrange("p (i r u) -> p i r u", i=2, u=2)
+            nc.scalar.copy(out=dst, in_=bank[:].rearrange("p i u r -> p i r u"))
+
+        def quantize(codes, scales, grouped):
+            nc.vector.quantize_mx(out=codes.bitcast(FP8X4), scales=scales, in_=grouped.rearrange("p c j -> p (c j)"))
+
+        def prepare_x(b):
+            gx = work.tile([P, 512, 4], BF16, name="gx", tag="g2048", bufs=3, align_bytes=64)
+            for h in range(2):
+                turn([x_sb[b][:, 2 * h + i, :] for i in range(2)], gx[:, 256 * h : 256 * (h + 1), :])
+            quantize(xq[:, 512 * b : 512 * (b + 1)], xs[:, 512 * b : 512 * (b + 1)], gx[:])
+
+        def prepare_w(u):
+            for c in (1, 0, 2):
+                gw = work.tile([P, 256, 4], BF16, name="gw", tag="g1024", bufs=6, align_bytes=64)
+                turn([w_sb[u][:, i, 512 * c : 512 * (c + 1)] for i in range(2)], gw[:])
+                quantize(wq[:, c, 256 * u : 256 * (u + 1)], ws[:, c, 256 * u : 256 * (u + 1)], gw[:])
+
+        def prepare_t(b, it):
+            gt = work.tile([P, 512, 4], BF16, name="gt", tag="g2048", bufs=3, align_bytes=64)
+            for k in range(2):
+                turn([t_sb[b][it][:, k, 512 * G : 512 * (G + 1)] for G in range(2)], gt[:, 256 * k : 256 * (k + 1), :])
+            quantize(tq[b][:, 512 * it : 512 * (it + 1)], ts[b][:, 512 * it : 512 * (it + 1)], gt[:])
+
+        def windows(b, G, half, s1, pre, older):
+            tt = (2 * half, 2 * half + 1)
+            rows = slice(512 * b, 512 * (b + 1))
+            y = {}
+            for c in (1, 0, 2):
+                for t in tt:
+                    cols = slice(512 * G + P * t, 512 * G + P * (t + 1))
+                    y[c, t] = psum.tile([P, 512], BANK_DT, name="y%d" % c, tag="bank")
+                    nc.tensor.matmul_mx(
+                        out=y[c, t][:],
+                        lhsT=wq[:, c, cols].bitcast(FP8X4),
+                        lhsT_scale=ws[:, c, cols],
+                        rhs=xq[:, rows].bitcast(FP8X4),
+                        rhs_scale=xs[:, rows],
+                        start=True,
+                        stop=True,
+                    )
+            for t in tt:
+                nc.scalar.copy(out=y1_sb[t][:, 0:512], in_=y[1, t][:])
+            if older:
+                interleave_on_scalar(older[2], older[3])
+            for t in tt:
+                nc.vector.scalar_tensor_tensor(
+                    out=s1[:, t, :], in0=y[0, t][:], scalar=br[:, G, t : t + 1], in1=y1_sb[t][:, 1:513], op0=ADD, op1=ADD
+                )
+            for t in tt:
+                nc.vector.tensor_tensor(out=pre[:, t, 1:512], in0=y[2, t][:, 0:511], in1=s1[:, t, 1:512], op=ADD)
+
+        def interleave_on_vector(pre, hg):
+            nc.vector.tensor_scalar_max(out=hg[:, 0:SPLIT, :], in0=pre[:, :, 0:SPLIT].rearrange("p t j -> p j t"), scalar1=0.0)
+
+        def interleave_on_scalar(pre, hg):
+            nc.scalar.activation(out=hg[:, SPLIT:512, :], in_=pre[:, :, SPLIT:512].rearrange("p t j -> p j t"), func=RELU)
+
+        tiles_done = [0]
+
+        def scores(b, it):
+            staged = work.tile([P, 512, 2], F32, name="staged", tag="staged", bufs=4)
+            for jh in range(2):
+                js = slice(256 * jh, 256 * (jh + 1))
+                sc = psum.tile([P, 2, 256], F32, name="sc", tag="bank")
+                for k in range(2):
+                    for G in range(2):
+                        c0 = 512 * it + 256 * k + P * G
+                        nc.tensor.matmul_mx(
+                            out=sc[:, k, :],
+                            lhsT=tq[b][:, c0 : c0 + P].bitcast(FP8X4),
+                            lhsT_scale=ts[b][:, c0 : c0 + P],
+                            rhs=hq[b][:, G, js].bitcast(FP8X4),
+                            rhs_scale=hs[b][:, G, js],
+                            start=(G == 0),
+                            stop=(G == 1),
+                        )
+                n = tiles_done[0]
+                tiles_done[0] = n + 1
+                if n % 3 == 2 and n < 12:
+                    for k in range(2):
+                        nc.scalar.activation(out=staged[:, js, k], in_=sc[:, k, :], func=IDENTITY, bias=bb[:, k : k + 1])
+                    nc.scalar.dma_start(out=out[b, it * P : (it + 1) * P, js, :], in_=staged[:, js, :])
+                else:
+                    nc.vector.tensor_tensor(out=staged[:, js, :], in0=sc[:].rearrange("p k j -> p j k"), in1=bias2[:], op=ADD)
+                    nc.sync.dma_start(out=out[b, it * P : (it + 1) * P, js, :], in_=staged[:, js, :])
+
+        units = [(12, prepare_w, (u,)) for u in (1, 2, 3)] + [(8, prepare_x, (1,))]
+        units += [(8, prepare_t, (b, it)) for b in range(2) for it in range(4)]
+        runs = [[]]
+        for unit in units:
+            if sum(u[0] for u in runs[-1]) + unit[0] > MAX_RUN:
+                runs.append([])
+            runs[-1].append(unit)
+        assert len(runs) == 8
+
+        prepare_x(0)
+        prepare_w(0)
+        older = None
+        for pair in range(8):
+            b, G, half = pair // 4, (pair // 2) % 2, pair % 2
+            for count, prepare, args in runs[pair]:
+                prepare(*args)
+            if older:
+                interleave_on_vector(older[2], older[3])
+            if half == 0:
+                s1 = work.tile([P, 4, 512], F32, name="s1", tag="s1")
+                pre = work.tile([P, 4, 512], BF16, name="pre", tag="pre")
+            windows(b, G, half, s1, pre, older)
+            if older:
+                quantize(hq[older[0]][:, older[1], :], hs[older[0]][:, older[1], :], older[3][:])
+            older = None
+            if half == 1:
+                nc.vector.tensor_copy(out=pre[:, :, 0], in_=s1[:, :, 0])
+                hg = work.tile([P, 512, 4], BF16, name="hg", tag="hg", align_bytes=64)
+                older = (b, G, pre, hg)
+        scores(0, 0)
+        interleave_on_vector(older[2], older[3])
+        interleave_on_scalar(older[2], older[3])
+        scores(0, 1)
+        quantize(hq[1][:, 1, :], hs[1][:, 1, :], older[3][:])
+        scores(0, 2)
+        scores(0, 3)
+        for it in range(4):
+            scores(1, it)

@@ -14,7 +14,7 @@ IDENTITY = mybir.ActivationFunctionType.Identity
 
 P = 128
 FLOPS = 3 * 2 * 1024 * 1024 * 512 + 2 * 2 * 1024 * 512 * 1024
-MAX_RUN = 16
+RUN = 3
 SPLIT = 256
 
 BANK_DT = BF16
@@ -98,23 +98,36 @@ def tile_bilinearpairedlayer_pb_kernel(tc, t_bil, x_r, W_r, b_r, b_bil, out):
         def quantize(codes, scales, grouped):
             nc.vector.quantize_mx(out=codes.bitcast(FP8X4), scales=scales, in_=grouped.rearrange("p c j -> p (c j)"))
 
-        def prepare_x(b):
-            gx = work.tile([P, 512, 4], BF16, name="gx", tag="g2048", bufs=3, align_bytes=64)
-            for h in range(2):
-                turn([x_sb[b][:, 2 * h + i, :] for i in range(2)], gx[:, 256 * h : 256 * (h + 1), :])
-            quantize(xq[:, 512 * b : 512 * (b + 1)], xs[:, 512 * b : 512 * (b + 1)], gx[:])
+        open_tile = {}
+        hold_back = [False]
+        late = []
 
-        def prepare_w(u):
-            for c in (1, 0, 2):
-                gw = work.tile([P, 256, 4], BF16, name="gw", tag="g1024", bufs=6, align_bytes=64)
-                turn([w_sb[u][:, i, 512 * c : 512 * (c + 1)] for i in range(2)], gw[:])
-                quantize(wq[:, c, 256 * u : 256 * (u + 1)], ws[:, c, 256 * u : 256 * (u + 1)], gw[:])
+        def unit_x(b, h):
+            if h == 0:
+                open_tile["x"] = work.tile([P, 512, 4], BF16, name="gx", tag="g2048", bufs=3, align_bytes=64)
+            gx = open_tile["x"]
+            turn([x_sb[b][:, 2 * h + i, :] for i in range(2)], gx[:, 256 * h : 256 * (h + 1), :])
+            if h == 1:
+                quantize(xq[:, 512 * b : 512 * (b + 1)], xs[:, 512 * b : 512 * (b + 1)], gx[:])
 
-        def prepare_t(b, it):
-            gt = work.tile([P, 512, 4], BF16, name="gt", tag="g2048", bufs=3, align_bytes=64)
-            for k in range(2):
-                turn([t_sb[b][it][:, k, 512 * G : 512 * (G + 1)] for G in range(2)], gt[:, 256 * k : 256 * (k + 1), :])
+        def unit_w(u, c):
+            gw = work.tile([P, 256, 4], BF16, name="gw", tag="g1024", bufs=6, align_bytes=64)
+            turn([w_sb[u][:, i, 512 * c : 512 * (c + 1)] for i in range(2)], gw[:])
+            quantize(wq[:, c, 256 * u : 256 * (u + 1)], ws[:, c, 256 * u : 256 * (u + 1)], gw[:])
+
+        def quantize_t(b, it, gt):
             quantize(tq[b][:, 512 * it : 512 * (it + 1)], ts[b][:, 512 * it : 512 * (it + 1)], gt[:])
+
+        def unit_t(b, it, k):
+            if k == 0:
+                open_tile["t"] = work.tile([P, 512, 4], BF16, name="gt", tag="g2048", bufs=3, align_bytes=64)
+            gt = open_tile["t"]
+            turn([t_sb[b][it][:, k, 512 * G : 512 * (G + 1)] for G in range(2)], gt[:, 256 * k : 256 * (k + 1), :])
+            if k == 1:
+                if hold_back[0]:
+                    late.append((b, it, gt))
+                else:
+                    quantize_t(b, it, gt)
 
         def windows(b, G, half, s1, pre, older):
             tt = (2 * half, 2 * half + 1)
@@ -136,7 +149,7 @@ def tile_bilinearpairedlayer_pb_kernel(tc, t_bil, x_r, W_r, b_r, b_bil, out):
             for t in tt:
                 nc.scalar.copy(out=y1_sb[t][:, 0:512], in_=y[1, t][:])
             if older:
-                interleave_on_scalar(older[2], older[3])
+                interleave_on_scalar(older[2], older[3], SPLIT)
             for t in tt:
                 nc.vector.scalar_tensor_tensor(
                     out=s1[:, t, :], in0=y[0, t][:], scalar=br[:, G, t : t + 1], in1=y1_sb[t][:, 1:513], op0=ADD, op1=ADD
@@ -144,59 +157,56 @@ def tile_bilinearpairedlayer_pb_kernel(tc, t_bil, x_r, W_r, b_r, b_bil, out):
             for t in tt:
                 nc.vector.tensor_tensor(out=pre[:, t, 1:512], in0=y[2, t][:, 0:511], in1=s1[:, t, 1:512], op=ADD)
 
-        def interleave_on_vector(pre, hg):
-            nc.vector.tensor_scalar_max(out=hg[:, 0:SPLIT, :], in0=pre[:, :, 0:SPLIT].rearrange("p t j -> p j t"), scalar1=0.0)
+        def interleave_on_vector(pre, hg, split):
+            nc.vector.tensor_scalar_max(out=hg[:, 0:split, :], in0=pre[:, :, 0:split].rearrange("p t j -> p j t"), scalar1=0.0)
 
-        def interleave_on_scalar(pre, hg):
-            nc.scalar.activation(out=hg[:, SPLIT:512, :], in_=pre[:, :, SPLIT:512].rearrange("p t j -> p j t"), func=RELU)
+        def interleave_on_scalar(pre, hg, split):
+            nc.scalar.activation(out=hg[:, split:512, :], in_=pre[:, :, split:512].rearrange("p t j -> p j t"), func=RELU)
 
-        tiles_done = [0]
+        staged_now = {}
 
-        def scores(b, it):
-            staged = work.tile([P, 512, 2], F32, name="staged", tag="staged", bufs=4)
-            for jh in range(2):
-                js = slice(256 * jh, 256 * (jh + 1))
-                sc = psum.tile([P, 2, 256], F32, name="sc", tag="bank")
+        def score_tile(b, it, jh, on_scalar):
+            if jh == 0:
+                staged_now[0] = work.tile([P, 512, 2], F32, name="staged", tag="staged", bufs=4)
+            staged = staged_now[0]
+            js = slice(256 * jh, 256 * (jh + 1))
+            sc = psum.tile([P, 2, 256], F32, name="sc", tag="bank")
+            for k in range(2):
+                for G in range(2):
+                    c0 = 512 * it + 256 * k + P * G
+                    nc.tensor.matmul_mx(
+                        out=sc[:, k, :],
+                        lhsT=tq[b][:, c0 : c0 + P].bitcast(FP8X4),
+                        lhsT_scale=ts[b][:, c0 : c0 + P],
+                        rhs=hq[b][:, G, js].bitcast(FP8X4),
+                        rhs_scale=hs[b][:, G, js],
+                        start=(G == 0),
+                        stop=(G == 1),
+                    )
+            if on_scalar:
                 for k in range(2):
-                    for G in range(2):
-                        c0 = 512 * it + 256 * k + P * G
-                        nc.tensor.matmul_mx(
-                            out=sc[:, k, :],
-                            lhsT=tq[b][:, c0 : c0 + P].bitcast(FP8X4),
-                            lhsT_scale=ts[b][:, c0 : c0 + P],
-                            rhs=hq[b][:, G, js].bitcast(FP8X4),
-                            rhs_scale=hs[b][:, G, js],
-                            start=(G == 0),
-                            stop=(G == 1),
-                        )
-                n = tiles_done[0]
-                tiles_done[0] = n + 1
-                if n % 3 == 2 and n < 12:
-                    for k in range(2):
-                        nc.scalar.activation(out=staged[:, js, k], in_=sc[:, k, :], func=IDENTITY, bias=bb[:, k : k + 1])
-                    nc.scalar.dma_start(out=out[b, it * P : (it + 1) * P, js, :], in_=staged[:, js, :])
-                else:
-                    nc.vector.tensor_tensor(out=staged[:, js, :], in0=sc[:].rearrange("p k j -> p j k"), in1=bias2[:], op=ADD)
-                    nc.sync.dma_start(out=out[b, it * P : (it + 1) * P, js, :], in_=staged[:, js, :])
+                    nc.scalar.activation(out=staged[:, js, k], in_=sc[:, k, :], func=IDENTITY, bias=bb[:, k : k + 1])
+                nc.scalar.dma_start(out=out[b, it * P : (it + 1) * P, js, :], in_=staged[:, js, :])
+            else:
+                nc.vector.tensor_tensor(out=staged[:, js, :], in0=sc[:].rearrange("p k j -> p j k"), in1=bias2[:], op=ADD)
+                nc.sync.dma_start(out=out[b, it * P : (it + 1) * P, js, :], in_=staged[:, js, :])
 
-        units = [(12, prepare_w, (u,)) for u in (1, 2, 3)] + [(8, prepare_x, (1,))]
-        units += [(8, prepare_t, (b, it)) for b in range(2) for it in range(4)]
-        runs = [[]]
-        for unit in units:
-            if sum(u[0] for u in runs[-1]) + unit[0] > MAX_RUN:
-                runs.append([])
-            runs[-1].append(unit)
-        assert len(runs) == 8
+        units = [(unit_w, (u, c)) for u in (1, 2, 3) for c in (1, 0, 2)] + [(unit_x, (1, h)) for h in range(2)]
+        units += [(unit_t, (b, it, k)) for b in range(2) for it in range(4) for k in range(2)]
+        runs = [units[i : i + RUN] for i in range(0, len(units), RUN)]
+        assert len(runs) == 9
 
-        prepare_x(0)
-        prepare_w(0)
+        for h in range(2):
+            unit_x(0, h)
+        for c in (1, 0, 2):
+            unit_w(0, c)
         older = None
-        for pair in range(8):
-            b, G, half = pair // 4, (pair // 2) % 2, pair % 2
-            for count, prepare, args in runs[pair]:
-                prepare(*args)
+        for step in range(8):
+            b, G, half = step // 4, (step // 2) % 2, step % 2
+            for unit, args in runs[step]:
+                unit(*args)
             if older:
-                interleave_on_vector(older[2], older[3])
+                interleave_on_vector(older[2], older[3], SPLIT)
             if half == 0:
                 s1 = work.tile([P, 4, 512], F32, name="s1", tag="s1")
                 pre = work.tile([P, 4, 512], BF16, name="pre", tag="pre")
@@ -208,12 +218,18 @@ def tile_bilinearpairedlayer_pb_kernel(tc, t_bil, x_r, W_r, b_r, b_bil, out):
                 nc.vector.tensor_copy(out=pre[:, :, 0], in_=s1[:, :, 0])
                 hg = work.tile([P, 512, 4], BF16, name="hg", tag="hg", align_bytes=64)
                 older = (b, G, pre, hg)
-        scores(0, 0)
-        interleave_on_vector(older[2], older[3])
-        interleave_on_scalar(older[2], older[3])
-        scores(0, 1)
-        quantize(hq[1][:, 1, :], hs[1][:, 1, :], older[3][:])
-        scores(0, 2)
-        scores(0, 3)
-        for it in range(4):
-            scores(1, it)
+
+        hold_back[0] = True
+        for unit, args in runs[8]:
+            unit(*args)
+        tiles = [(b, it, jh) for b in range(2) for it in range(4) for jh in range(2)]
+        for n in range(16):
+            if n == 2:
+                interleave_on_vector(older[2], older[3], SPLIT)
+                interleave_on_scalar(older[2], older[3], SPLIT)
+            if n == 4:
+                quantize(hq[1][:, 1, :], hs[1][:, 1, :], older[3][:])
+                for b, it, gt in late:
+                    quantize_t(b, it, gt)
+            b, it, jh = tiles[n]
+            score_tile(b, it, jh, n % 3 == 2 and n < 12)

@@ -46,8 +46,7 @@ def tile_bilinearpairedlayer_pb_kernel(tc, t_bil, x_r, W_r, b_r, b_bil, out):
             nc.sync.dma_start(out=t_sb[b][it][:], in_=t_bil[b, it * P : (it + 1) * P])
 
         load_x(0)
-        load_w(0, [slice(512 * c, 512 * (c + 1)) for c in (1, 0, 2)])
-        for u in (1, 2, 3):
+        for u in range(4):
             load_w(u, [slice(0, 1536)])
         load_x(1)
         for b in range(2):

@@ -14,6 +14,7 @@ IDENTITY = mybir.ActivationFunctionType.Identity
 
 P = 128
 FLOPS = 3 * 2 * 1024 * 1024 * 512 + 2 * 2 * 1024 * 512 * 1024
+BIAS_LOAD_STEP = 5
 RUN = 3
 SPLIT = 256
 
@@ -55,9 +56,8 @@ def tile_bilinearpairedlayer_pb_kernel(tc, t_bil, x_r, W_r, b_r, b_bil, out):
 
         br = keep.tile([P, 2, 4], BF16, name="br")
         bb = keep.tile([P, 2], BF16, name="bb")
-        with nc.allow_non_contiguous_dma(reason="two small bias vectors"):
+        with nc.allow_non_contiguous_dma(reason="a small bias vector"):
             nc.scalar.dma_start(out=br[:], in_=b_r.rearrange("(G p t) -> p G t", G=2, t=4))
-            nc.scalar.dma_start(out=bb[:], in_=b_bil.partition_broadcast(P))
 
         warm = keep.tile([P, 2], F32, name="warm")
         nc.vector.memset(warm[:], 0.0)
@@ -69,8 +69,6 @@ def tile_bilinearpairedlayer_pb_kernel(tc, t_bil, x_r, W_r, b_r, b_bil, out):
         zero = keep.tile([P, 256], F32, name="zero")
         nc.gpsimd.memset(zero[:], 0.0)
         bias2 = keep.tile([P, 256, 2], F32, name="bias2")
-        for k in range(2):
-            nc.gpsimd.tensor_scalar(out=bias2[:, :, k], in0=zero[:], scalar1=bb[:, k : k + 1], scalar2=None, op0=ADD)
 
         y1_sb = [keep.tile([P, 520], BANK_DT, name="y1_sb%d" % n) for n in range(4)]
         for n in range(4):
@@ -217,6 +215,12 @@ def tile_bilinearpairedlayer_pb_kernel(tc, t_bil, x_r, W_r, b_r, b_bil, out):
                 nc.vector.tensor_copy(out=pre[:, :, 0], in_=s1[:, :, 0])
                 hg = work.tile([P, 512, 4], BF16, name="hg", tag="hg", align_bytes=64)
                 older = (b, G, pre, hg)
+            if step == BIAS_LOAD_STEP:
+                with nc.allow_non_contiguous_dma(reason="a small bias vector"):
+                    nc.scalar.dma_start(out=bb[:], in_=b_bil.partition_broadcast(P))
+            if step == BIAS_LOAD_STEP + 2:
+                for k in range(2):
+                    nc.scalar.activation(out=bias2[:, :, k], in_=zero[:], func=IDENTITY, bias=bb[:, k : k + 1])
 
         hold_back[0] = True
         for unit, args in runs[8]:

@@ -31,28 +31,29 @@ def tile_bilinearpairedlayer_pb_kernel(tc, t_bil, x_r, W_r, b_r, b_bil, out):
 
         x_sb = [keep.tile([P, 4, 512], BF16, name="x_sb%d" % b) for b in range(2)]
         w_sb = [keep.tile([P, 2, 1536], BF16, name="w_sb%d" % u) for u in range(4)]
-        t_sb = [[keep.tile([P, 2, 1024], BF16, name="t_sb%d%d" % (b, it)) for it in range(4)] for b in range(2)]
+        t_sb = [[keep.tile([P, 2, 2, 1024], BF16, name="t_sb%d%d" % (b, pair)) for pair in range(2)] for b in range(2)]
         w_view = W_r.rearrange("(G m h t) c -> G h m t c", G=2, m=P, h=2, t=2)
 
-        def load_x(b):
-            x_view = x_r[b].rearrange("(r p) f -> p r f", p=P)
-            for h in range(2):
-                nc.sync.dma_start(out=x_sb[b][:, 2 * h : 2 * h + 2, :], in_=x_view[:, 2 * h : 2 * h + 2, :])
+        def load_x(b, pieces):
+            x_view = x_r[b].rearrange("(p r) f -> p r f", r=4)
+            for rs in pieces:
+                nc.sync.dma_start(out=x_sb[b][:, rs, :], in_=x_view[:, rs, :])
 
         def load_w(u, pieces):
             for cs in pieces:
                 nc.sync.dma_start(out=w_sb[u][:, :, cs], in_=w_view[u // 2, u % 2][:, :, cs])
 
-        def load_t(b, it):
-            nc.sync.dma_start(out=t_sb[b][it][:], in_=t_bil[b, it * P : (it + 1) * P])
+        def load_t(b, pair):
+            rows = t_bil[b, 2 * pair * P : 2 * (pair + 1) * P]
+            nc.sync.dma_start(out=t_sb[b][pair][:], in_=rows.rearrange("(a p) k g -> p a k g", p=P))
 
-        load_x(0)
+        load_x(0, [slice(0, 2), slice(2, 4)])
         for u in range(4):
             load_w(u, [slice(0, 1536)])
-        load_x(1)
+        load_x(1, [slice(0, 4)])
         for b in range(2):
-            for it in range(4):
-                load_t(b, it)
+            for pair in range(2):
+                load_t(b, pair)
 
         br = keep.tile([P, 2, 4], BF16, name="br")
         bb = keep.tile([P, 2], BF16, name="bb")
@@ -83,12 +84,16 @@ def tile_bilinearpairedlayer_pb_kernel(tc, t_bil, x_r, W_r, b_r, b_bil, out):
         hq = [keep.tile([P, 2, 512], U32, name="hq%d" % b, align_bytes=64) for b in range(2)]
         hs = [keep.tile([P, 2, 512], U8, name="hs%d" % b, align_bytes=64) for b in range(2)]
 
-        def turn(blocks, grouped):
+        def turn_into_bank(blocks):
             bank = psum.tile([P, 2, 2, P], F32, name="turned", tag="bank")
             for i in range(2):
                 words = blocks[i].bitcast(F32)
                 for u in range(2):
                     nc.tensor.transpose(bank[:, i, u, :], words[:, u:256:2], ident[:])
+            return bank
+
+        def turn(blocks, grouped):
+            bank = turn_into_bank(blocks)
             dst = grouped.rearrange("p c j -> p (c j)").bitcast(F32).rearrange("p (i r u) -> p i r u", i=2, u=2)
             nc.scalar.copy(out=dst, in_=bank[:].rearrange("p i u r -> p i r u"))
 
@@ -103,7 +108,9 @@ def tile_bilinearpairedlayer_pb_kernel(tc, t_bil, x_r, W_r, b_r, b_bil, out):
             if h == 0:
                 open_tile["x"] = work.tile([P, 512, 4], BF16, name="gx", tag="g2048", bufs=3, align_bytes=64)
             gx = open_tile["x"]
-            turn([x_sb[b][:, 2 * h + i, :] for i in range(2)], gx[:, 256 * h : 256 * (h + 1), :])
+            bank = turn_into_bank([x_sb[b][:, 2 * h + i, :] for i in range(2)])
+            dst = gx[:].rearrange("p c j -> p (c j)").bitcast(F32).rearrange("p (r g i u) -> p g r i u", g=2, i=2, u=2)
+            nc.scalar.copy(out=dst[:, h], in_=bank[:].rearrange("p i u r -> p r i u"))
             if h == 1:
                 quantize(xq[:, 512 * b : 512 * (b + 1)], xs[:, 512 * b : 512 * (b + 1)], gx[:])
 
@@ -119,7 +126,7 @@ def tile_bilinearpairedlayer_pb_kernel(tc, t_bil, x_r, W_r, b_r, b_bil, out):
             if k == 0:
                 open_tile["t"] = work.tile([P, 512, 4], BF16, name="gt", tag="g2048", bufs=3, align_bytes=64)
             gt = open_tile["t"]
-            turn([t_sb[b][it][:, k, 512 * G : 512 * (G + 1)] for G in range(2)], gt[:, 256 * k : 256 * (k + 1), :])
+            turn([t_sb[b][it // 2][:, it % 2, k, 512 * G : 512 * (G + 1)] for G in range(2)], gt[:, 256 * k : 256 * (k + 1), :])
             if k == 1:
                 if hold_back[0]:
                     late.append((b, it, gt))

@@ -171,7 +171,7 @@ def tile_bilinearpairedlayer_pb_kernel(tc, t_bil, x_r, W_r, b_r, b_bil, out):
 
         def score_tile(b, it, jh, on_scalar):
             if jh == 0:
-                staged_now[0] = work.tile([P, 512, 2], F32, name="staged", tag="staged", bufs=4)
+                staged_now[0] = work.tile([P, 512, 2], F32, name="staged", tag="staged", bufs=8)
             staged = staged_now[0]
             js = slice(256 * jh, 256 * (jh + 1))
             sc = psum.tile([P, 2, 256], F32, name="sc", tag="bank")
@@ -190,10 +190,12 @@ def tile_bilinearpairedlayer_pb_kernel(tc, t_bil, x_r, W_r, b_r, b_bil, out):
             if on_scalar:
                 for k in range(2):
                     nc.scalar.activation(out=staged[:, js, k], in_=sc[:, k, :], func=IDENTITY, bias=bb[:, k : k + 1])
-                nc.scalar.dma_start(out=out[b, it * P : (it + 1) * P, js, :], in_=staged[:, js, :])
             else:
                 nc.vector.tensor_tensor(out=staged[:, js, :], in0=sc[:].rearrange("p k j -> p j k"), in1=bias2[:], op=ADD)
+            if (b, it) == (1, 3):
                 nc.sync.dma_start(out=out[b, it * P : (it + 1) * P, js, :], in_=staged[:, js, :])
+            elif jh == 1:
+                nc.sync.dma_start(out=out[b, it * P : (it + 1) * P], in_=staged[:])
 
         units = [(unit_w, (u, c)) for u in (1, 2, 3) for c in (1, 0, 2)] + [(unit_x, (1, h)) for h in range(2)]
         units += [(unit_t, (b, it, k)) for b in range(2) for it in range(4) for k in range(2)]

@@ -47,18 +47,20 @@ def tile_bilinearpairedlayer_pb_kernel(tc, t_bil, x_r, W_r, b_r, b_bil, out):
             rows = t_bil[b, 2 * pair * P : 2 * (pair + 1) * P]
             nc.sync.dma_start(out=t_sb[b][pair][:], in_=rows.rearrange("(a p) k g -> p a k g", p=P))
 
-        load_x(0, [slice(0, 2), slice(2, 4)])
-        for u in range(4):
+        load_x(0, [slice(0, 4)])
+        for u in range(2):
+            load_w(u, [slice(0, 1536)])
+        br = keep.tile([P, 2, 4], BF16, name="br")
+        with nc.allow_non_contiguous_dma(reason="a small bias vector"):
+            nc.sync.dma_start(out=br[:], in_=b_r.rearrange("(G p t) -> p G t", G=2, t=4))
+        for u in range(2, 4):
             load_w(u, [slice(0, 1536)])
         load_x(1, [slice(0, 4)])
         for b in range(2):
             for pair in range(2):
                 load_t(b, pair)
 
-        br = keep.tile([P, 2, 4], BF16, name="br")
         bb = keep.tile([P, 2], BF16, name="bb")
-        with nc.allow_non_contiguous_dma(reason="a small bias vector"):
-            nc.scalar.dma_start(out=br[:], in_=b_r.rearrange("(G p t) -> p G t", G=2, t=4))
 
         warm = keep.tile([P, 2], F32, name="warm")
         nc.vector.memset(warm[:], 0.0)

from contextlib import ExitStack

import concourse.mybir as mybir
from concourse.masks import make_identity

F32 = mybir.dt.float32
BF16 = mybir.dt.bfloat16
U32 = mybir.dt.uint32
U8 = mybir.dt.uint8
FP8X4 = mybir.dt.float8_e4m3fn_x4
ADD = mybir.AluOpType.add
RELU = mybir.ActivationFunctionType.Relu
IDENTITY = mybir.ActivationFunctionType.Identity

P = 128
FLOPS = 3 * 2 * 1024 * 1024 * 512 + 2 * 2 * 1024 * 512 * 1024
BIAS_LOAD_STEP = 5
RUN = 3
SPLIT = 256

BANK_DT = BF16


def tile_bilinearpairedlayer_pb_kernel(tc, t_bil, x_r, W_r, b_r, b_bil, out):
    nc = tc.nc
    with ExitStack() as ctx:
        keep = ctx.enter_context(tc.tile_pool(name="keep", bufs=1))
        work = ctx.enter_context(tc.tile_pool(name="work", bufs=2))
        psum = ctx.enter_context(tc.psum_pool(name="psum", bufs=8))
        ctx.enter_context(tc.manual_schedule())

        x_sb = [keep.tile([P, 4, 512], BF16, name="x_sb%d" % b) for b in range(2)]
        w_sb = [keep.tile([P, 2, 1536], BF16, name="w_sb%d" % u) for u in range(4)]
        t_sb = [[keep.tile([P, 2, 2, 1024], BF16, name="t_sb%d%d" % (b, pair)) for pair in range(2)] for b in range(2)]
        w_view = W_r.rearrange("(G m h t) c -> G h m t c", G=2, m=P, h=2, t=2)

        def load_x(b, pieces):
            x_view = x_r[b].rearrange("(p r) f -> p r f", r=4)
            for rs in pieces:
                nc.sync.dma_start(out=x_sb[b][:, rs, :], in_=x_view[:, rs, :])

        def load_w(u, pieces):
            for cs in pieces:
                nc.sync.dma_start(out=w_sb[u][:, :, cs], in_=w_view[u // 2, u % 2][:, :, cs])

        def load_t(b, pair):
            rows = t_bil[b, 2 * pair * P : 2 * (pair + 1) * P]
            nc.sync.dma_start(out=t_sb[b][pair][:], in_=rows.rearrange("(a p) k g -> p a k g", p=P))

        load_x(0, [slice(0, 4)])
        for u in range(2):
            load_w(u, [slice(0, 1536)])
        br = keep.tile([P, 2, 4], BF16, name="br")
        with nc.allow_non_contiguous_dma(reason="a small bias vector"):
            nc.sync.dma_start(out=br[:], in_=b_r.rearrange("(G p t) -> p G t", G=2, t=4))
        for u in range(2, 4):
            load_w(u, [slice(0, 1536)])
        load_x(1, [slice(0, 4)])
        for b in range(2):
            for pair in range(2):
                load_t(b, pair)

        bb = keep.tile([P, 2], BF16, name="bb")

        warm = keep.tile([P, 2], F32, name="warm")
        nc.vector.memset(warm[:], 0.0)
        nc.scalar.activation(out=warm[:, 1:2], in_=warm[:, 0:1], func=RELU)

        ident = keep.tile([P, P], F32, name="ident")
        make_identity(nc, ident[:])

        zero = keep.tile([P, 256], F32, name="zero")
        nc.gpsimd.memset(zero[:], 0.0)
        bias2 = keep.tile([P, 256, 2], F32, name="bias2")

        y1_sb = [keep.tile([P, 520], BANK_DT, name="y1_sb%d" % n) for n in range(4)]
        for n in range(4):
            nc.vector.memset(y1_sb[n][:, 512:520], 0.0)

        xq = keep.tile([P, 1024], U32, name="xq", align_bytes=64)
        xs = keep.tile([P, 1024], U8, name="xs", align_bytes=64)
        wq = keep.tile([P, 3, 1024], U32, name="wq", align_bytes=64)
        ws = keep.tile([P, 3, 1024], U8, name="ws", align_bytes=64)
        tq = [keep.tile([P, 2048], U32, name="tq%d" % b, align_bytes=64) for b in range(2)]
        ts = [keep.tile([P, 2048], U8, name="ts%d" % b, align_bytes=64) for b in range(2)]
        hq = [keep.tile([P, 2, 512], U32, name="hq%d" % b, align_bytes=64) for b in range(2)]
        hs = [keep.tile([P, 2, 512], U8, name="hs%d" % b, align_bytes=64) for b in range(2)]

        def turn_into_bank(blocks):
            bank = psum.tile([P, 2, 2, P], F32, name="turned", tag="bank")
            for i in range(2):
                words = blocks[i].bitcast(F32)
                for u in range(2):
                    nc.tensor.transpose(bank[:, i, u, :], words[:, u:256:2], ident[:])
            return bank

        def turn(blocks, grouped):
            bank = turn_into_bank(blocks)
            dst = grouped.rearrange("p c j -> p (c j)").bitcast(F32).rearrange("p (i r u) -> p i r u", i=2, u=2)
            nc.scalar.copy(out=dst, in_=bank[:].rearrange("p i u r -> p i r u"))

        def quantize(codes, scales, grouped):
            nc.vector.quantize_mx(out=codes.bitcast(FP8X4), scales=scales, in_=grouped.rearrange("p c j -> p (c j)"))

        open_tile = {}
        hold_back = [False]
        late = []

        def unit_x(b, h):
            if h == 0:
                open_tile["x"] = work.tile([P, 512, 4], BF16, name="gx", tag="g2048", bufs=3, align_bytes=64)
            gx = open_tile["x"]
            bank = turn_into_bank([x_sb[b][:, 2 * h + i, :] for i in range(2)])
            dst = gx[:].rearrange("p c j -> p (c j)").bitcast(F32).rearrange("p (r g i u) -> p g r i u", g=2, i=2, u=2)
            nc.scalar.copy(out=dst[:, h], in_=bank[:].rearrange("p i u r -> p r i u"))
            if h == 1:
                quantize(xq[:, 512 * b : 512 * (b + 1)], xs[:, 512 * b : 512 * (b + 1)], gx[:])

        def unit_w(u, c):
            gw = work.tile([P, 256, 4], BF16, name="gw", tag="g1024", bufs=6, align_bytes=64)
            turn([w_sb[u][:, i, 512 * c : 512 * (c + 1)] for i in range(2)], gw[:])
            quantize(wq[:, c, 256 * u : 256 * (u + 1)], ws[:, c, 256 * u : 256 * (u + 1)], gw[:])

        def quantize_t(b, it, gt):
            quantize(tq[b][:, 512 * it : 512 * (it + 1)], ts[b][:, 512 * it : 512 * (it + 1)], gt[:])

        def unit_t(b, it, k):
            if k == 0:
                open_tile["t"] = work.tile([P, 512, 4], BF16, name="gt", tag="g2048", bufs=3, align_bytes=64)
            gt = open_tile["t"]
            turn([t_sb[b][it // 2][:, it % 2, k, 512 * G : 512 * (G + 1)] for G in range(2)], gt[:, 256 * k : 256 * (k + 1), :])
            if k == 1:
                if hold_back[0]:
                    late.append((b, it, gt))
                else:
                    quantize_t(b, it, gt)

        def windows(b, G, half, s1, pre, older):
            tt = (2 * half, 2 * half + 1)
            rows = slice(512 * b, 512 * (b + 1))
            y = {}
            for c in (1, 0, 2):
                for t in tt:
                    cols = slice(512 * G + P * t, 512 * G + P * (t + 1))
                    y[c, t] = psum.tile([P, 512], BANK_DT, name="y%d" % c, tag="bank")
                    nc.tensor.matmul_mx(
                        out=y[c, t][:],
                        lhsT=wq[:, c, cols].bitcast(FP8X4),
                        lhsT_scale=ws[:, c, cols],
                        rhs=xq[:, rows].bitcast(FP8X4),
                        rhs_scale=xs[:, rows],
                        start=True,
                        stop=True,
                    )
            for t in tt:
                nc.scalar.copy(out=y1_sb[t][:, 0:512], in_=y[1, t][:])
            if older:
                interleave_on_scalar(older[2], older[3], SPLIT)
            for t in tt:
                nc.vector.scalar_tensor_tensor(
                    out=s1[:, t, :], in0=y[0, t][:], scalar=br[:, G, t : t + 1], in1=y1_sb[t][:, 1:513], op0=ADD, op1=ADD
                )
            for t in tt:
                nc.vector.tensor_tensor(out=pre[:, t, 1:512], in0=y[2, t][:, 0:511], in1=s1[:, t, 1:512], op=ADD)

        def interleave_on_vector(pre, hg, split):
            nc.vector.tensor_scalar_max(out=hg[:, 0:split, :], in0=pre[:, :, 0:split].rearrange("p t j -> p j t"), scalar1=0.0)

        def interleave_on_scalar(pre, hg, split):
            nc.scalar.activation(out=hg[:, split:512, :], in_=pre[:, :, split:512].rearrange("p t j -> p j t"), func=RELU)

        staged_now = {}

        def score_tile(b, it, jh, on_scalar):
            if jh == 0:
                staged_now[0] = work.tile([P, 512, 2], F32, name="staged", tag="staged", bufs=8)
            staged = staged_now[0]
            js = slice(256 * jh, 256 * (jh + 1))
            sc = psum.tile([P, 2, 256], F32, name="sc", tag="bank")
            for k in range(2):
                for G in range(2):
                    c0 = 512 * it + 256 * k + P * G
                    nc.tensor.matmul_mx(
                        out=sc[:, k, :],
                        lhsT=tq[b][:, c0 : c0 + P].bitcast(FP8X4),
                        lhsT_scale=ts[b][:, c0 : c0 + P],
                        rhs=hq[b][:, G, js].bitcast(FP8X4),
                        rhs_scale=hs[b][:, G, js],
                        start=(G == 0),
                        stop=(G == 1),
                    )
            if on_scalar:
                for k in range(2):
                    nc.scalar.activation(out=staged[:, js, k], in_=sc[:, k, :], func=IDENTITY, bias=bb[:, k : k + 1])
            else:
                nc.vector.tensor_tensor(out=staged[:, js, :], in0=sc[:].rearrange("p k j -> p j k"), in1=bias2[:], op=ADD)
            if (b, it) == (1, 3):
                nc.sync.dma_start(out=out[b, it * P : (it + 1) * P, js, :], in_=staged[:, js, :])
            elif jh == 1:
                nc.sync.dma_start(out=out[b, it * P : (it + 1) * P], in_=staged[:])

        units = [(unit_w, (u, c)) for u in (1, 2, 3) for c in (1, 0, 2)] + [(unit_x, (1, h)) for h in range(2)]
        units += [(unit_t, (b, it, k)) for b in range(2) for it in range(4) for k in range(2)]
        runs = [units[i : i + RUN] for i in range(0, len(units), RUN)]
        assert len(runs) == 9

        for h in range(2):
            unit_x(0, h)
        for c in (1, 0, 2):
            unit_w(0, c)
        older = None
        for step in range(8):
            b, G, half = step // 4, (step // 2) % 2, step % 2
            for unit, args in runs[step]:
                unit(*args)
            if older:
                interleave_on_vector(older[2], older[3], SPLIT)
            if half == 0:
                s1 = work.tile([P, 4, 512], F32, name="s1", tag="s1")
                pre = work.tile([P, 4, 512], BF16, name="pre", tag="pre")
            windows(b, G, half, s1, pre, older)
            if older:
                quantize(hq[older[0]][:, older[1], :], hs[older[0]][:, older[1], :], older[3][:])
            older = None
            if half == 1:
                nc.vector.tensor_copy(out=pre[:, :, 0], in_=s1[:, :, 0])
                hg = work.tile([P, 512, 4], BF16, name="hg", tag="hg", align_bytes=64)
                older = (b, G, pre, hg)
            if step == BIAS_LOAD_STEP:
                with nc.allow_non_contiguous_dma(reason="a small bias vector"):
                    nc.scalar.dma_start(out=bb[:], in_=b_bil.partition_broadcast(P))
            if step == BIAS_LOAD_STEP + 2:
                for k in range(2):
                    nc.scalar.activation(out=bias2[:, :, k], in_=zero[:], func=IDENTITY, bias=bb[:, k : k + 1])

        hold_back[0] = True
        for unit, args in runs[8]:
            unit(*args)
        tiles = [(b, it, jh) for b in range(2) for it in range(4) for jh in range(2)]
        for n in range(16):
            if n == 2:
                interleave_on_vector(older[2], older[3], SPLIT)
                interleave_on_scalar(older[2], older[3], SPLIT)
            if n == 4:
                quantize(hq[1][:, 1, :], hs[1][:, 1, :], older[3][:])
                for b, it, gt in late:
                    quantize_t(b, it, gt)
            b, it, jh = tiles[n]
            score_tile(b, it, jh, n % 3 == 2 and n < 12)
